import numpy as np
import ml_dtypes


def mxq(x, axis, fmt="e4m3"):
    dtype, down = {"e4m3": (ml_dtypes.float8_e4m3fn, 7), "e5m2": (ml_dtypes.float8_e5m2, 14)}[fmt]
    v = np.moveaxis(np.asarray(x, np.float32).astype(ml_dtypes.bfloat16).astype(np.float64), axis, -1)
    blocks = v.reshape(v.shape[:-1] + (-1, 32))
    amax = np.abs(blocks).max(-1, keepdims=True)
    byte = np.maximum(np.where(amax > 0, np.frexp(amax)[1] - 1 + 127, 0) - down, 1)
    scale = np.exp2(byte - 127.0)
    codes = (blocks / scale).astype(np.float32).astype(dtype).astype(np.float64)
    return np.moveaxis((codes * scale).reshape(v.shape), -1, axis)


WIDE = False


def mx_kscale(k):
    if not WIDE:
        return np.ones(k)
    levels = np.array([10, -10, 5, -5, 0])
    if k % 512:
        return np.exp2(np.random.permutation(np.resize(levels, k // 32))).repeat(32)
    a = np.empty((k // 512, 16))
    for p in range(k // 512):
        a[p, :8] = np.random.permutation(np.resize(levels, 8))
        for g in range(8):
            far = levels[np.abs(levels - a[p, g]) >= 10]
            a[p, g + 8] = far[np.random.randint(len(far))]
    return np.exp2(a.ravel()).repeat(32)


BF16 = ml_dtypes.bfloat16


def bf(x):
    return np.asarray(x, np.float32).astype(BF16)


def f64(x):
    return np.asarray(x).astype(np.float64)


H, N, S, T, L, K = 2, 2, 128, 512, 1024, 512
NH = N * H


def rel_shift(p):
    zero_pad = np.zeros((NH, S, 1))
    padded = np.concatenate([zero_pad, p], axis=2)
    padded = padded.reshape(NH, T + 1, S)
    return padded[:, 1:, :].reshape(NH, S, T)


def setup_inputs():
    s = mx_kscale(K)
    return {"queries": bf(np.random.standard_normal((NH, S, K)) * s),
            "v_bias": bf(np.random.standard_normal((1, H, 1, K)) / np.sqrt(K) * s),
            "R": bf(np.random.standard_normal((H, L, K)) / s)}


def reference(queries, v_bias, R):
    q = (f64(queries) * K ** -0.5).reshape(N, H, S, K)
    q_v = q + f64(v_bias)
    r = f64(R)[:, :T, :]
    pos = mxq(q_v, 3, "e4m3") @ mxq(r, 2, "e4m3").transpose(0, 2, 1)
    return rel_shift(pos.reshape(NH, S, T))

@@ -1,0 +1,150 @@
+import concourse.mybir as mybir
+from concourse.masks import make_identity
+
+F32 = mybir.dt.float32
+BF16 = mybir.dt.bfloat16
+U32 = mybir.dt.uint32
+U8 = mybir.dt.uint8
+FP8X4 = mybir.dt.float8_e4m3fn_x4
+MULT = mybir.AluOpType.mult
+ADD = mybir.AluOpType.add
+
+P = 128
+SEQS = 2
+HEADS = 2
+BATCHES = SEQS * HEADS
+S = 128
+T = 512
+K = 512
+PACK = 4
+HALVES = 2
+T_CHUNK = 256
+CHUNKS = T // T_CHUNK
+ROWS_EACH = T_CHUNK // P
+PADDED = T + 1
+PITCH = 520
+DROPPED = S
+SMALL_ROWS = 16
+
+FLOPS = 2 * BATCHES * S * T * K
+BYTES = 2 * (BATCHES * S * K + HEADS * K + HEADS * T * K) + 4 * BATCHES * S * T
+
+
+def tile_relativepositionsdpa_pa_s_kernel(tc, queries, v_bias, R, out):
+    nc = tc.nc
+    with tc.tile_pool(name="keep", bufs=1) as keep, tc.psum_pool(
+        name="transposed", bufs=4
+    ) as transposed, tc.psum_pool(name="scores", bufs=4) as scores:
+        bias_rows = keep.tile([P, K], BF16, name="bias_rows")
+        nc.vector.memset(bias_rows[:], 0.0)
+        nc.sync.dma_start(
+            out=bias_rows[0:HEADS, :],
+            in_=v_bias.rearrange("o h i k -> (o h i) k"),
+        )
+        q_by_head = queries.rearrange("(n h) s k -> h s n k", h=HEADS)
+        q_raw = keep.tile([P, HEADS, SEQS, K], BF16, name="q_raw")
+        r_raw = keep.tile([P, HEADS, CHUNKS, ROWS_EACH * K], BF16, name="r_raw")
+        for h in range(HEADS):
+            nc.sync.dma_start(out=q_raw[:, h, :, :], in_=q_by_head[h])
+            for c in range(CHUNKS):
+                nc.sync.dma_start(
+                    out=r_raw[:, h, c, :].rearrange("p (a k) -> p a k", a=ROWS_EACH),
+                    in_=R[h, c * T_CHUNK : (c + 1) * T_CHUNK, :].rearrange("(a r) k -> r a k", a=ROWS_EACH),
+                )
+
+        identity = keep.tile([P, P], F32, name="identity")
+        make_identity(nc, identity[:])
+
+
+        padded = keep.tile([P, BATCHES, PITCH], F32, name="padded")
+        nc.gpsimd.memset(padded[:, :, 0:8], 0.0)
+
+        q_grouped = keep.tile([P, HEADS, SEQS * S, PACK], BF16, name="q_grouped", align_bytes=64)
+        r_grouped = keep.tile([P, HEADS, T * PACK], BF16, name="r_grouped", align_bytes=64)
+        q_codes = keep.tile([P, HEADS, SEQS, S], U32, name="q_codes", align_bytes=64)
+        q_scales = keep.tile([P, HEADS, SEQS, S], U8, name="q_scales", align_bytes=64)
+        r_codes = keep.tile([P, HEADS, T], U32, name="r_codes", align_bytes=64)
+        r_scales = keep.tile([P, HEADS, T], U8, name="r_scales", align_bytes=64)
+
+        bias_t = transposed.tile([P, HALVES, P], F32, tag="t", name="bias_t")
+        for u in range(HALVES):
+            nc.tensor.transpose(bias_t[:, u, :], bias_rows[:].bitcast(F32)[:, u::HALVES], identity[:])
+        bias_words = keep.tile([P, HEADS * HALVES], F32, name="bias_words")
+        nc.vector.tensor_copy(
+            out=bias_words[:].rearrange("p (h u) -> p h u", u=HALVES),
+            in_=bias_t[:, :, 0:HEADS].rearrange("p u h -> p h u"),
+        )
+        bias_values = bias_words[:].bitcast(BF16)
+
+        out_flat = out.rearrange("b s t -> b (s t)")
+
+        def store_rows(first, end, batches):
+            nc.sync.dma_start(
+                out=out_flat[batches, first * PADDED - DROPPED : end * PADDED - DROPPED].rearrange(
+                    "b (s c) -> s b c", c=PADDED
+                ),
+                in_=padded[first:end, batches, 0:PADDED],
+            )
+
+        for h in range(HEADS):
+            q_t = transposed.tile([P, HALVES, SEQS, S], F32, tag="t", name="q_t%d" % h)
+            for n in range(SEQS):
+                q_words = q_raw[:, h, n, :].bitcast(F32)
+                for u in range(HALVES):
+                    nc.tensor.transpose(q_t[:, u, n, :], q_words[:, u::HALVES], identity[:])
+            for u in range(HALVES):
+                first = h * PACK + u * 2
+                nc.vector.scalar_tensor_tensor(
+                    out=q_grouped[:, h, :, u * 2 : u * 2 + 2],
+                    in0=q_t[:, u, :, :].rearrange("p n s -> p (n s)").bitcast(BF16).rearrange("p (g e) -> p g e", e=2),
+                    scalar=K**-0.5,
+                    in1=bias_values[:, first : first + 2].unsqueeze(1).to_broadcast([P, SEQS * S, 2]),
+                    op0=MULT,
+                    op1=ADD,
+                )
+            nc.vector.quantize_mx(
+                out=q_codes[:, h, :, :].rearrange("p n s -> p (n s)").bitcast(FP8X4),
+                scales=q_scales[:, h, :, :].rearrange("p n s -> p (n s)"),
+                in_=q_grouped[:, h, :, :].rearrange("p g t -> p (g t)"),
+            )
+
+            for c in range(CHUNKS):
+                cols = slice(c * T_CHUNK, (c + 1) * T_CHUNK)
+                r_words = r_raw[:, h, c, :].bitcast(F32).rearrange("p (a w) -> p a w", a=ROWS_EACH)
+                r_t = transposed.tile([P, ROWS_EACH, HALVES, P], F32, tag="t", name="r_t%d_%d" % (h, c))
+                for a in range(ROWS_EACH):
+                    for u in range(HALVES):
+                        nc.tensor.transpose(r_t[:, a, u, :], r_words[:, a, u::HALVES], identity[:])
+                piece = r_grouped[:, h, c * T_CHUNK * PACK : (c + 1) * T_CHUNK * PACK]
+                nc.scalar.copy(
+                    out=piece.bitcast(F32).rearrange("p (a r u) -> p a r u", a=ROWS_EACH, u=HALVES),
+                    in_=r_t[:].rearrange("p a u r -> p a r u"),
+                )
+                nc.vector.quantize_mx(
+                    out=r_codes[:, h, cols].bitcast(FP8X4), scales=r_scales[:, h, cols], in_=piece
+                )
+                for n in range(SEQS):
+                    b = n * HEADS + h
+                    pos = scores.tile([P, T_CHUNK], F32, tag="pos", name="pos%d_%d" % (b, c))
+                    nc.tensor.matmul_mx(
+                        out=pos[:],
+                        lhsT=q_codes[:, h, n, :].bitcast(FP8X4),
+                        lhsT_scale=q_scales[:, h, n, :],
+                        rhs=r_codes[:, h, cols].bitcast(FP8X4),
+                        rhs_scale=r_scales[:, h, cols],
+                        start=True,
+                        stop=True,
+                    )
+                    first = 1 + c * T_CHUNK
+                    if n == 0:
+                        nc.vector.tensor_copy(out=padded[:, b, first : first + T_CHUNK], in_=pos[:])
+                    else:
+                        nc.scalar.copy(out=padded[:, b, first : first + T_CHUNK], in_=pos[:])
+
+            of_head = slice(h, BATCHES, HEADS)
+            store_rows(SMALL_ROWS, S, of_head)
+            store_rows(1, SMALL_ROWS, of_head)
+            nc.sync.dma_start(
+                out=out_flat[of_head, 0 : PADDED - DROPPED].unsqueeze(0),
+                in_=padded[0:1, of_head, DROPPED:PADDED],
+            )

@@ -17,14 +17,20 @@ S = 128
 T = 512
 K = 512
 PACK = 4
-HALVES = 2
+PAIR = 2
 T_CHUNK = 256
 CHUNKS = T // T_CHUNK
 ROWS_EACH = T_CHUNK // P
 PADDED = T + 1
-PITCH = 520
 DROPPED = S
-SMALL_ROWS = 16
+
+GROUPS = 16
+DUOS = 4
+ROWS = 2
+GROUP = DUOS * ROWS * PADDED
+BLOCK = 8
+SPILL = 6
+PITCH = ROWS * PADDED + SPILL
 
 FLOPS = 2 * BATCHES * S * T * K
 BYTES = 2 * (BATCHES * S * K + HEADS * K + HEADS * T * K) + 4 * BATCHES * S * T
@@ -34,18 +40,16 @@ def tile_relativepositionsdpa_pa_s_kernel(tc, queries, v_bias, R, out):
     nc = tc.nc
     with tc.tile_pool(name="keep", bufs=1) as keep, tc.psum_pool(
         name="transposed", bufs=4
-    ) as transposed, tc.psum_pool(name="scores", bufs=4) as scores:
+    ) as transposed, tc.psum_pool(name="scores", bufs=3) as scores, tc.psum_pool(name="spills", bufs=1) as spills:
         bias_rows = keep.tile([P, K], BF16, name="bias_rows")
-        nc.vector.memset(bias_rows[:], 0.0)
-        nc.sync.dma_start(
-            out=bias_rows[0:HEADS, :],
-            in_=v_bias.rearrange("o h i k -> (o h i) k"),
-        )
-        q_by_head = queries.rearrange("(n h) s k -> h s n k", h=HEADS)
-        q_raw = keep.tile([P, HEADS, SEQS, K], BF16, name="q_raw")
+        nc.vector.memset(bias_rows[:].bitcast(F32), 0.0)
+        q_pairs = queries.rearrange("(n h) (q a) k -> h q n (a k)", h=HEADS, a=ROWS)
+        q_raw = keep.tile([P, HEADS, ROWS * K], BF16, name="q_raw")
         r_raw = keep.tile([P, HEADS, CHUNKS, ROWS_EACH * K], BF16, name="r_raw")
         for h in range(HEADS):
-            nc.sync.dma_start(out=q_raw[:, h, :, :], in_=q_by_head[h])
+            nc.sync.dma_start(out=q_raw[:, h, :], in_=q_pairs[h])
+            if h == 0:
+                nc.sync.dma_start(out=bias_rows[0:HEADS, :], in_=v_bias.rearrange("o h i k -> (o h i) k"))
             for c in range(CHUNKS):
                 nc.sync.dma_start(
                     out=r_raw[:, h, c, :].rearrange("p (a k) -> p a k", a=ROWS_EACH),
@@ -54,97 +58,125 @@ def tile_relativepositionsdpa_pa_s_kernel(tc, queries, v_bias, R, out):
 
         identity = keep.tile([P, P], F32, name="identity")
         make_identity(nc, identity[:])
+        perm = keep.tile([P, P], F32, name="perm")
+        nc.vector.tensor_copy(
+            out=perm[:].rearrange("p (g n r) -> p g n r", n=SEQS, r=DUOS),
+            in_=identity[:].rearrange("p (g r n) -> p g n r", n=SEQS, r=DUOS),
+        )
 
+        padded = keep.tile([P, HEADS, PITCH], F32, name="padded")
+        for j in range(ROWS + 1):
+            nc.vector.memset(padded[:, :, j * PADDED : j * PADDED + 1], 0.0)
 
-        padded = keep.tile([P, BATCHES, PITCH], F32, name="padded")
-        nc.gpsimd.memset(padded[:, :, 0:8], 0.0)
-
-        q_grouped = keep.tile([P, HEADS, SEQS * S, PACK], BF16, name="q_grouped", align_bytes=64)
+        q_grouped = keep.tile([P, HEADS, ROWS * P, PACK], BF16, name="q_grouped", align_bytes=64)
+        next_grouped = keep.tile([P, HEADS, P * PACK], BF16, name="next_grouped", align_bytes=64)
         r_grouped = keep.tile([P, HEADS, T * PACK], BF16, name="r_grouped", align_bytes=64)
-        q_codes = keep.tile([P, HEADS, SEQS, S], U32, name="q_codes", align_bytes=64)
-        q_scales = keep.tile([P, HEADS, SEQS, S], U8, name="q_scales", align_bytes=64)
+        q_codes = keep.tile([P, HEADS, ROWS + 1, P], U32, name="q_codes", align_bytes=64)
+        q_scales = keep.tile([P, HEADS, ROWS + 1, P], U8, name="q_scales", align_bytes=64)
         r_codes = keep.tile([P, HEADS, T], U32, name="r_codes", align_bytes=64)
         r_scales = keep.tile([P, HEADS, T], U8, name="r_scales", align_bytes=64)
 
-        bias_t = transposed.tile([P, HALVES, P], F32, tag="t", name="bias_t")
-        for u in range(HALVES):
-            nc.tensor.transpose(bias_t[:, u, :], bias_rows[:].bitcast(F32)[:, u::HALVES], identity[:])
-        bias_words = keep.tile([P, HEADS * HALVES], F32, name="bias_words")
+        bias_t = transposed.tile([P, PAIR, P], F32, tag="t", name="bias_t")
+        for u in range(PAIR):
+            nc.tensor.transpose(bias_t[:, u, :], bias_rows[:].bitcast(F32)[:, u::PAIR], identity[:])
+        bias_words = keep.tile([P, HEADS * PAIR], F32, name="bias_words")
         nc.vector.tensor_copy(
-            out=bias_words[:].rearrange("p (h u) -> p h u", u=HALVES),
+            out=bias_words[:].rearrange("p (h u) -> p h u", u=PAIR),
             in_=bias_t[:, :, 0:HEADS].rearrange("p u h -> p h u"),
         )
         bias_values = bias_words[:].bitcast(BF16)
 
-        out_flat = out.rearrange("b s t -> b (s t)")
+        out_seqs = out.rearrange("(n h) s t -> n (h s t)", h=HEADS)
+        origins = (DROPPED, 0)
+        views = []
+        for h in range(HEADS):
+            first = h * S * T - DROPPED + origins[h]
+            views.append(out_seqs[:, first : first + GROUPS * GROUP].rearrange("n (g c) -> g n c", c=GROUP))
 
-        def store_rows(first, end, batches):
-            nc.sync.dma_start(
-                out=out_flat[batches, first * PADDED - DROPPED : end * PADDED - DROPPED].rearrange(
-                    "b (s c) -> s b c", c=PADDED
-                ),
-                in_=padded[first:end, batches, 0:PADDED],
-            )
+        def store(h, r, first, end, g=0):
+            to = r * ROWS * PADDED + first - origins[h]
+            shift = 0
+            if to < 0:
+                to = to + GROUP
+                shift = 1
+            for n in range(SEQS):
+                nc.sync.dma_start(
+                    out=views[h][g - shift : GROUPS - shift, n, to : to + end - first],
+                    in_=padded[(g * SEQS + n) * DUOS + r :: SEQS * DUOS, h, first:end],
+                )
 
         for h in range(HEADS):
-            q_t = transposed.tile([P, HALVES, SEQS, S], F32, tag="t", name="q_t%d" % h)
-            for n in range(SEQS):
-                q_words = q_raw[:, h, n, :].bitcast(F32)
-                for u in range(HALVES):
-                    nc.tensor.transpose(q_t[:, u, n, :], q_words[:, u::HALVES], identity[:])
-            for u in range(HALVES):
-                first = h * PACK + u * 2
-                nc.vector.scalar_tensor_tensor(
-                    out=q_grouped[:, h, :, u * 2 : u * 2 + 2],
-                    in0=q_t[:, u, :, :].rearrange("p n s -> p (n s)").bitcast(BF16).rearrange("p (g e) -> p g e", e=2),
-                    scalar=K**-0.5,
-                    in1=bias_values[:, first : first + 2].unsqueeze(1).to_broadcast([P, SEQS * S, 2]),
-                    op0=MULT,
-                    op1=ADD,
-                )
+            q_t = transposed.tile([P, ROWS, P, PAIR], F32, tag="t", name="q_t%d" % h)
+            for a in range(ROWS):
+                q_words = q_raw[:, h, a * K : (a + 1) * K].bitcast(F32)
+                for u in range(PAIR):
+                    nc.tensor.transpose(q_t[:, a, :, u], q_words[:, u::PAIR], perm[:])
+            nc.vector.scalar_tensor_tensor(
+                out=q_grouped[:, h, :, :],
+                in0=q_t[:].rearrange("p a c u -> p (a c u)").bitcast(BF16).rearrange("p (g t) -> p g t", t=PACK),
+                scalar=K**-0.5,
+                in1=bias_values[:, h * PACK : (h + 1) * PACK].unsqueeze(1).to_broadcast([P, ROWS * P, PACK]),
+                op0=MULT,
+                op1=ADD,
+            )
             nc.vector.quantize_mx(
-                out=q_codes[:, h, :, :].rearrange("p n s -> p (n s)").bitcast(FP8X4),
-                scales=q_scales[:, h, :, :].rearrange("p n s -> p (n s)"),
+                out=q_codes[:, h, 0:ROWS, :].rearrange("p a c -> p (a c)").bitcast(FP8X4),
+                scales=q_scales[:, h, 0:ROWS, :].rearrange("p a c -> p (a c)"),
                 in_=q_grouped[:, h, :, :].rearrange("p g t -> p (g t)"),
             )
+            nc.vector.tensor_copy(
+                out=next_grouped[:, h, :], in_=q_grouped[:, h, 1 : P + 1, :].rearrange("p g t -> p (g t)")
+            )
+            nc.vector.quantize_mx(
+                out=q_codes[:, h, ROWS, :].bitcast(FP8X4), scales=q_scales[:, h, ROWS, :], in_=next_grouped[:, h, :]
+            )
+            pos = [scores.tile([P, T], F32, tag="pos", name="pos%d_%d" % (h, a)) for a in range(ROWS)]
 
             for c in range(CHUNKS):
                 cols = slice(c * T_CHUNK, (c + 1) * T_CHUNK)
                 r_words = r_raw[:, h, c, :].bitcast(F32).rearrange("p (a w) -> p a w", a=ROWS_EACH)
-                r_t = transposed.tile([P, ROWS_EACH, HALVES, P], F32, tag="t", name="r_t%d_%d" % (h, c))
-                for a in range(ROWS_EACH):
-                    for u in range(HALVES):
-                        nc.tensor.transpose(r_t[:, a, u, :], r_words[:, a, u::HALVES], identity[:])
+                r_t = transposed.tile([P, ROWS_EACH, P, PAIR], F32, tag="t", name="r_t%d_%d" % (h, c))
+                for i in range(ROWS_EACH):
+                    for u in range(PAIR):
+                        nc.tensor.transpose(r_t[:, i, :, u], r_words[:, i, u::PAIR], identity[:])
                 piece = r_grouped[:, h, c * T_CHUNK * PACK : (c + 1) * T_CHUNK * PACK]
                 nc.scalar.copy(
-                    out=piece.bitcast(F32).rearrange("p (a r u) -> p a r u", a=ROWS_EACH, u=HALVES),
-                    in_=r_t[:].rearrange("p a u r -> p a r u"),
+                    out=piece.bitcast(F32), in_=r_t[:].rearrange("p a r u -> p (a r u)"),
                 )
                 nc.vector.quantize_mx(
                     out=r_codes[:, h, cols].bitcast(FP8X4), scales=r_scales[:, h, cols], in_=piece
                 )
-                for n in range(SEQS):
-                    b = n * HEADS + h
-                    pos = scores.tile([P, T_CHUNK], F32, tag="pos", name="pos%d_%d" % (b, c))
+                for a in range(ROWS):
                     nc.tensor.matmul_mx(
-                        out=pos[:],
-                        lhsT=q_codes[:, h, n, :].bitcast(FP8X4),
-                        lhsT_scale=q_scales[:, h, n, :],
+                        out=pos[a][:, cols],
+                        lhsT=q_codes[:, h, a, :].bitcast(FP8X4),
+                        lhsT_scale=q_scales[:, h, a, :],
                         rhs=r_codes[:, h, cols].bitcast(FP8X4),
                         rhs_scale=r_scales[:, h, cols],
                         start=True,
                         stop=True,
                     )
-                    first = 1 + c * T_CHUNK
-                    if n == 0:
-                        nc.vector.tensor_copy(out=padded[:, b, first : first + T_CHUNK], in_=pos[:])
+                    first = a * PADDED + 1 + c * T_CHUNK
+                    if a == 0:
+                        nc.vector.tensor_copy(out=padded[:, h, first : first + T_CHUNK], in_=pos[a][:, cols])
                     else:
-                        nc.scalar.copy(out=padded[:, b, first : first + T_CHUNK], in_=pos[:])
+                        nc.scalar.copy(out=padded[:, h, first : first + T_CHUNK], in_=pos[a][:, cols])
+                if c == 0:
+                    spill = spills.tile([P, 64], F32, tag="spill", name="spill%d" % h)
+                    nc.tensor.matmul_mx(
+                        out=spill[:],
+                        lhsT=q_codes[:, h, ROWS, :].bitcast(FP8X4),
+                        lhsT_scale=q_scales[:, h, ROWS, :],
+                        rhs=r_codes[:, h, 0:64].bitcast(FP8X4),
+                        rhs_scale=r_scales[:, h, 0:64],
+                        start=True,
+                        stop=True,
+                    )
+                    first = ROWS * PADDED + 1
+                    nc.scalar.copy(out=padded[:, h, first:PITCH], in_=spill[:, 0 : PITCH - first])
+                    store(h, 0, 0, DROPPED, g=1)
 
-            of_head = slice(h, BATCHES, HEADS)
-            store_rows(SMALL_ROWS, S, of_head)
-            store_rows(1, SMALL_ROWS, of_head)
-            nc.sync.dma_start(
-                out=out_flat[of_head, 0 : PADDED - DROPPED].unsqueeze(0),
-                in_=padded[0:1, of_head, DROPPED:PADDED],
-            )
+            for r in range(DUOS):
+                begin = DROPPED if r == 0 else -(r * ROWS * PADDED) % BLOCK
+                end = ROWS * PADDED + -((r + 1) * ROWS * PADDED) % BLOCK
+                store(h, r, begin, end)

@@ -38,9 +38,9 @@ BYTES = 2 * (BATCHES * S * K + HEADS * K + HEADS * T * K) + 4 * BATCHES * S * T
 
 def tile_relativepositionsdpa_pa_s_kernel(tc, queries, v_bias, R, out):
     nc = tc.nc
-    with tc.tile_pool(name="keep", bufs=1) as keep, tc.psum_pool(
+    with tc.manual_schedule(), tc.tile_pool(name="keep", bufs=1) as keep, tc.psum_pool(
         name="transposed", bufs=4
-    ) as transposed, tc.psum_pool(name="scores", bufs=3) as scores, tc.psum_pool(name="spills", bufs=1) as spills:
+    ) as transposed, tc.psum_pool(name="scores", bufs=4) as scores:
         bias_rows = keep.tile([P, K], BF16, name="bias_rows")
         nc.vector.memset(bias_rows[:].bitcast(F32), 0.0)
         q_pairs = queries.rearrange("(n h) (q a) k -> h q n (a k)", h=HEADS, a=ROWS)
@@ -60,8 +60,8 @@ def tile_relativepositionsdpa_pa_s_kernel(tc, queries, v_bias, R, out):
         make_identity(nc, identity[:])
         perm = keep.tile([P, P], F32, name="perm")
         nc.vector.tensor_copy(
-            out=perm[:].rearrange("p (g n r) -> p g n r", n=SEQS, r=DUOS),
-            in_=identity[:].rearrange("p (g r n) -> p g n r", n=SEQS, r=DUOS),
+            out=perm[:].rearrange("p (r g n) -> p r g n", n=SEQS, r=DUOS),
+            in_=identity[:].rearrange("p (g r n) -> p r g n", n=SEQS, r=DUOS),
         )
 
         padded = keep.tile([P, HEADS, PITCH], F32, name="padded")
@@ -69,10 +69,11 @@ def tile_relativepositionsdpa_pa_s_kernel(tc, queries, v_bias, R, out):
             nc.vector.memset(padded[:, :, j * PADDED : j * PADDED + 1], 0.0)
 
         q_grouped = keep.tile([P, HEADS, ROWS * P, PACK], BF16, name="q_grouped", align_bytes=64)
-        next_grouped = keep.tile([P, HEADS, P * PACK], BF16, name="next_grouped", align_bytes=64)
         r_grouped = keep.tile([P, HEADS, T * PACK], BF16, name="r_grouped", align_bytes=64)
-        q_codes = keep.tile([P, HEADS, ROWS + 1, P], U32, name="q_codes", align_bytes=64)
-        q_scales = keep.tile([P, HEADS, ROWS + 1, P], U8, name="q_scales", align_bytes=64)
+        q_codes = keep.tile([P, HEADS, ROWS * P], U32, name="q_codes", align_bytes=64)
+        next_codes = keep.tile([P, P], U32, name="next_codes", align_bytes=64)
+        next_scales = keep.tile([P, P], U8, name="next_scales", align_bytes=64)
+        q_scales = keep.tile([P, HEADS, ROWS * P], U8, name="q_scales", align_bytes=64)
         r_codes = keep.tile([P, HEADS, T], U32, name="r_codes", align_bytes=64)
         r_scales = keep.tile([P, HEADS, T], U8, name="r_scales", align_bytes=64)
 
@@ -86,97 +87,168 @@ def tile_relativepositionsdpa_pa_s_kernel(tc, queries, v_bias, R, out):
         )
         bias_values = bias_words[:].bitcast(BF16)
 
-        out_seqs = out.rearrange("(n h) s t -> n (h s t)", h=HEADS)
-        origins = (DROPPED, 0)
-        views = []
-        for h in range(HEADS):
-            first = h * S * T - DROPPED + origins[h]
-            views.append(out_seqs[:, first : first + GROUPS * GROUP].rearrange("n (g c) -> g n c", c=GROUP))
+        out_all = out.rearrange("b s t -> (b s t)")
+        RUN = ROWS * PADDED
 
-        def store(h, r, first, end, g=0):
-            to = r * ROWS * PADDED + first - origins[h]
-            shift = 0
-            if to < 0:
-                to = to + GROUP
-                shift = 1
-            for n in range(SEQS):
-                nc.sync.dma_start(
-                    out=views[h][g - shift : GROUPS - shift, n, to : to + end - first],
-                    in_=padded[(g * SEQS + n) * DUOS + r :: SEQS * DUOS, h, first:end],
-                )
+        def runs(b, first, count, pitch):
+            first = first + b * S * T
+            return out_all[first : first + count * pitch].rearrange("(q c) -> q c", c=pitch)
 
-        for h in range(HEADS):
+        def store_plain(n):
+            b = n * HEADS
+            nc.sync.dma_start(out=runs(b, 0, S // ROWS, RUN)[:, 0 : RUN - DROPPED], in_=padded[n::SEQS, 0, DROPPED:RUN])
+
+        def store_plain_front(n):
+            b = n * HEADS
+            nc.sync.dma_start(
+                out=runs(b, RUN - DROPPED, S // ROWS - 1, RUN)[:, 0:DROPPED],
+                in_=padded[SEQS + n :: SEQS, 0, 0:DROPPED],
+            )
+
+        def store_blocks(queue, n, r):
+            b = n * HEADS + 1
+            begin = DROPPED if r == 0 else -(r * RUN) % BLOCK
+            end = RUN + -((r + 1) * RUN) % BLOCK
+            at = r * RUN
+            queue.dma_start(
+                out=runs(b, -DROPPED, GROUPS, GROUP)[:, at + begin : at + end],
+                in_=padded[r * GROUPS * SEQS + n : (r + 1) * GROUPS * SEQS : SEQS, 1, begin:end],
+            )
+
+        def store_blocks_front(n):
+            b = n * HEADS + 1
+            nc.gpsimd.dma_start(
+                out=runs(b, GROUP - DROPPED, GROUPS - 1, GROUP)[:, 0:DROPPED],
+                in_=padded[SEQS + n : GROUPS * SEQS : SEQS, 1, 0:DROPPED],
+            )
+
+        q_ts = {}
+        r_ts = {}
+        poss = {}
+
+        def transpose_q(h):
             q_t = transposed.tile([P, ROWS, P, PAIR], F32, tag="t", name="q_t%d" % h)
             for a in range(ROWS):
                 q_words = q_raw[:, h, a * K : (a + 1) * K].bitcast(F32)
                 for u in range(PAIR):
-                    nc.tensor.transpose(q_t[:, a, :, u], q_words[:, u::PAIR], perm[:])
+                    nc.tensor.transpose(q_t[:, a, :, u], q_words[:, u::PAIR], (identity, perm)[h][:])
+            q_ts[h] = q_t
+
+        def form_q(h):
             nc.vector.scalar_tensor_tensor(
                 out=q_grouped[:, h, :, :],
-                in0=q_t[:].rearrange("p a c u -> p (a c u)").bitcast(BF16).rearrange("p (g t) -> p g t", t=PACK),
+                in0=q_ts[h][:].rearrange("p a c u -> p (a c u)").bitcast(BF16).rearrange("p (g t) -> p g t", t=PACK),
                 scalar=K**-0.5,
                 in1=bias_values[:, h * PACK : (h + 1) * PACK].unsqueeze(1).to_broadcast([P, ROWS * P, PACK]),
                 op0=MULT,
                 op1=ADD,
             )
+
+        def quantize_q(h):
             nc.vector.quantize_mx(
-                out=q_codes[:, h, 0:ROWS, :].rearrange("p a c -> p (a c)").bitcast(FP8X4),
-                scales=q_scales[:, h, 0:ROWS, :].rearrange("p a c -> p (a c)"),
+                out=q_codes[:, h, :].bitcast(FP8X4),
+                scales=q_scales[:, h, :],
                 in_=q_grouped[:, h, :, :].rearrange("p g t -> p (g t)"),
             )
-            nc.vector.tensor_copy(
-                out=next_grouped[:, h, :], in_=q_grouped[:, h, 1 : P + 1, :].rearrange("p g t -> p (g t)")
-            )
+
+        def transpose_r(h, c):
+            r_words = r_raw[:, h, c, :].bitcast(F32).rearrange("p (a w) -> p a w", a=ROWS_EACH)
+            r_t = transposed.tile([P, ROWS_EACH, P, PAIR], F32, tag="t", name="r_t%d_%d" % (h, c))
+            for i in range(ROWS_EACH):
+                for u in range(PAIR):
+                    nc.tensor.transpose(r_t[:, i, :, u], r_words[:, i, u::PAIR], identity[:])
+            r_ts[h, c] = r_t
+
+        def copy_r(h, c):
+            piece = r_grouped[:, h, c * T_CHUNK * PACK : (c + 1) * T_CHUNK * PACK]
+            nc.scalar.copy(out=piece.bitcast(F32), in_=r_ts[h, c][:].rearrange("p a r u -> p (a r u)"))
+
+        def quantize_r(h, c):
+            cols = slice(c * T_CHUNK, (c + 1) * T_CHUNK)
             nc.vector.quantize_mx(
-                out=q_codes[:, h, ROWS, :].bitcast(FP8X4), scales=q_scales[:, h, ROWS, :], in_=next_grouped[:, h, :]
+                out=r_codes[:, h, cols].bitcast(FP8X4),
+                scales=r_scales[:, h, cols],
+                in_=r_grouped[:, h, c * T_CHUNK * PACK : (c + 1) * T_CHUNK * PACK],
             )
-            pos = [scores.tile([P, T], F32, tag="pos", name="pos%d_%d" % (h, a)) for a in range(ROWS)]
 
-            for c in range(CHUNKS):
-                cols = slice(c * T_CHUNK, (c + 1) * T_CHUNK)
-                r_words = r_raw[:, h, c, :].bitcast(F32).rearrange("p (a w) -> p a w", a=ROWS_EACH)
-                r_t = transposed.tile([P, ROWS_EACH, P, PAIR], F32, tag="t", name="r_t%d_%d" % (h, c))
-                for i in range(ROWS_EACH):
-                    for u in range(PAIR):
-                        nc.tensor.transpose(r_t[:, i, :, u], r_words[:, i, u::PAIR], identity[:])
-                piece = r_grouped[:, h, c * T_CHUNK * PACK : (c + 1) * T_CHUNK * PACK]
-                nc.scalar.copy(
-                    out=piece.bitcast(F32), in_=r_t[:].rearrange("p a r u -> p (a r u)"),
-                )
-                nc.vector.quantize_mx(
-                    out=r_codes[:, h, cols].bitcast(FP8X4), scales=r_scales[:, h, cols], in_=piece
-                )
-                for a in range(ROWS):
-                    nc.tensor.matmul_mx(
-                        out=pos[a][:, cols],
-                        lhsT=q_codes[:, h, a, :].bitcast(FP8X4),
-                        lhsT_scale=q_scales[:, h, a, :],
-                        rhs=r_codes[:, h, cols].bitcast(FP8X4),
-                        rhs_scale=r_scales[:, h, cols],
-                        start=True,
-                        stop=True,
-                    )
-                    first = a * PADDED + 1 + c * T_CHUNK
-                    if a == 0:
-                        nc.vector.tensor_copy(out=padded[:, h, first : first + T_CHUNK], in_=pos[a][:, cols])
-                    else:
-                        nc.scalar.copy(out=padded[:, h, first : first + T_CHUNK], in_=pos[a][:, cols])
-                if c == 0:
-                    spill = spills.tile([P, 64], F32, tag="spill", name="spill%d" % h)
-                    nc.tensor.matmul_mx(
-                        out=spill[:],
-                        lhsT=q_codes[:, h, ROWS, :].bitcast(FP8X4),
-                        lhsT_scale=q_scales[:, h, ROWS, :],
-                        rhs=r_codes[:, h, 0:64].bitcast(FP8X4),
-                        rhs_scale=r_scales[:, h, 0:64],
-                        start=True,
-                        stop=True,
-                    )
-                    first = ROWS * PADDED + 1
-                    nc.scalar.copy(out=padded[:, h, first:PITCH], in_=spill[:, 0 : PITCH - first])
-                    store(h, 0, 0, DROPPED, g=1)
+        def multiply(out_tile, codes, scales, h, cols):
+            nc.tensor.matmul_mx(
+                out=out_tile,
+                lhsT=codes.bitcast(FP8X4),
+                lhsT_scale=scales,
+                rhs=r_codes[:, h, cols].bitcast(FP8X4),
+                rhs_scale=r_scales[:, h, cols],
+                start=True,
+                stop=True,
+            )
 
-            for r in range(DUOS):
-                begin = DROPPED if r == 0 else -(r * ROWS * PADDED) % BLOCK
-                end = ROWS * PADDED + -((r + 1) * ROWS * PADDED) % BLOCK
-                store(h, r, begin, end)
+        def score(h, c):
+            cols = slice(c * T_CHUNK, (c + 1) * T_CHUNK)
+            for a in range(ROWS):
+                pos = scores.tile([P, T], F32, tag="pos", name="pos%d_%d_%d" % (h, a, c))
+                poss[h, a, c] = pos
+                own = slice(a * P, (a + 1) * P)
+                multiply(pos[:, 0:T_CHUNK], q_codes[:, h, own], q_scales[:, h, own], h, cols)
+
+        def empty(copy, h, a, c):
+            first = a * PADDED + 1 + c * T_CHUNK
+            copy(out=padded[:, h, first : first + T_CHUNK], in_=poss[h, a, c][:, 0:T_CHUNK])
+
+        def quantize_next():
+            nc.vector.quantize_mx(
+                out=next_codes[:].bitcast(FP8X4),
+                scales=next_scales[:],
+                in_=q_grouped[:, 1, P // DUOS : P // DUOS + P, :].rearrange("p g t -> p (g t)"),
+            )
+
+        def score_next():
+            spill = transposed.tile([P, 64], F32, tag="t", name="spill")
+            poss[1] = spill
+            multiply(spill[:], next_codes[:], next_scales[:], 1, slice(0, 64))
+
+        def empty_spill():
+            first = ROWS * PADDED + 1
+            nc.scalar.copy(out=padded[:, 1, first:PITCH], in_=poss[1][:, 0 : PITCH - first])
+
+        transpose_q(0)
+        form_q(0)
+        transpose_r(0, 0)
+        copy_r(0, 0)
+        transpose_r(0, 1)
+        copy_r(0, 1)
+        quantize_q(0)
+        quantize_r(0, 0)
+        quantize_r(0, 1)
+        transpose_q(1)
+        form_q(1)
+        transpose_r(1, 0)
+        copy_r(1, 0)
+        score(0, 0)
+        empty(nc.scalar.copy, 0, 0, 0)
+        empty(nc.scalar.copy, 0, 1, 0)
+        store_plain_front(0)
+        store_plain_front(1)
+        transpose_r(1, 1)
+        copy_r(1, 1)
+        score(0, 1)
+        empty(nc.scalar.copy, 0, 0, 1)
+        empty(nc.scalar.copy, 0, 1, 1)
+        store_plain(0)
+        store_plain(1)
+        quantize_r(1, 0)
+        quantize_q(1)
+        quantize_r(1, 1)
+        quantize_next()
+        score(1, 0)
+        empty(nc.vector.tensor_copy, 1, 0, 0)
+        empty(nc.scalar.copy, 1, 1, 0)
+        store_blocks_front(0)
+        store_blocks_front(1)
+        score(1, 1)
+        score_next()
+        empty(nc.vector.tensor_copy, 1, 0, 1)
+        empty(nc.scalar.copy, 1, 1, 1)
+        empty_spill()
+        for r in range(DUOS):
+            store_blocks(nc.sync, 0, r)
+            store_blocks(nc.scalar, 1, r)

@@ -41,15 +41,24 @@ def tile_relativepositionsdpa_pa_s_kernel(tc, queries, v_bias, R, out):
     with tc.manual_schedule(), tc.tile_pool(name="keep", bufs=1) as keep, tc.psum_pool(
         name="transposed", bufs=4
     ) as transposed, tc.psum_pool(name="scores", bufs=4) as scores:
-        bias_rows = keep.tile([P, K], BF16, name="bias_rows")
-        nc.vector.memset(bias_rows[:].bitcast(F32), 0.0)
+        zeros = keep.tile([P, P], F32, name="zeros")
+        nc.vector.memset(zeros[:], 0.0)
+        warm = transposed.tile([P, T], F32, tag="t", name="warm")
+        nc.tensor.matmul(
+            out=warm[:].rearrange("p (i j) -> p i j", j=P),
+            lhsT=zeros[:],
+            rhs=zeros[:].unsqueeze(1).to_broadcast([P, T // P, P]),
+            start=True,
+            stop=True,
+        )
+        bias = keep.tile([P, HEADS, PACK], BF16, name="bias")
         q_pairs = queries.rearrange("(n h) (q a) k -> h q n (a k)", h=HEADS, a=ROWS)
         q_raw = keep.tile([P, HEADS, ROWS * K], BF16, name="q_raw")
         r_raw = keep.tile([P, HEADS, CHUNKS, ROWS_EACH * K], BF16, name="r_raw")
         for h in range(HEADS):
             nc.sync.dma_start(out=q_raw[:, h, :], in_=q_pairs[h])
             if h == 0:
-                nc.sync.dma_start(out=bias_rows[0:HEADS, :], in_=v_bias.rearrange("o h i k -> (o h i) k"))
+                nc.sync.dma_start(out=bias[:], in_=v_bias.rearrange("o h i (p t) -> p (o h i) t", t=PACK))
             for c in range(CHUNKS):
                 nc.sync.dma_start(
                     out=r_raw[:, h, c, :].rearrange("p (a k) -> p a k", a=ROWS_EACH),
@@ -76,16 +85,6 @@ def tile_relativepositionsdpa_pa_s_kernel(tc, queries, v_bias, R, out):
         q_scales = keep.tile([P, HEADS, ROWS * P], U8, name="q_scales", align_bytes=64)
         r_codes = keep.tile([P, HEADS, T], U32, name="r_codes", align_bytes=64)
         r_scales = keep.tile([P, HEADS, T], U8, name="r_scales", align_bytes=64)
-
-        bias_t = transposed.tile([P, PAIR, P], F32, tag="t", name="bias_t")
-        for u in range(PAIR):
-            nc.tensor.transpose(bias_t[:, u, :], bias_rows[:].bitcast(F32)[:, u::PAIR], identity[:])
-        bias_words = keep.tile([P, HEADS * PAIR], F32, name="bias_words")
-        nc.vector.tensor_copy(
-            out=bias_words[:].rearrange("p (h u) -> p h u", u=PAIR),
-            in_=bias_t[:, :, 0:HEADS].rearrange("p u h -> p h u"),
-        )
-        bias_values = bias_words[:].bitcast(BF16)
 
         out_all = out.rearrange("b s t -> (b s t)")
         RUN = ROWS * PADDED
@@ -139,7 +138,7 @@ def tile_relativepositionsdpa_pa_s_kernel(tc, queries, v_bias, R, out):
                 out=q_grouped[:, h, :, :],
                 in0=q_ts[h][:].rearrange("p a c u -> p (a c u)").bitcast(BF16).rearrange("p (g t) -> p g t", t=PACK),
                 scalar=K**-0.5,
-                in1=bias_values[:, h * PACK : (h + 1) * PACK].unsqueeze(1).to_broadcast([P, ROWS * P, PACK]),
+                in1=bias[:, h, :].unsqueeze(1).to_broadcast([P, ROWS * P, PACK]),
                 op0=MULT,
                 op1=ADD,
             )

@@ -61,8 +61,8 @@ def tile_relativepositionsdpa_pa_s_kernel(tc, queries, v_bias, R, out):
                 nc.sync.dma_start(out=bias[:], in_=v_bias.rearrange("o h i (p t) -> p (o h i) t", t=PACK))
             for c in range(CHUNKS):
                 nc.sync.dma_start(
-                    out=r_raw[:, h, c, :].rearrange("p (a k) -> p a k", a=ROWS_EACH),
-                    in_=R[h, c * T_CHUNK : (c + 1) * T_CHUNK, :].rearrange("(a r) k -> r a k", a=ROWS_EACH),
+                    out=r_raw[:, h, c, :],
+                    in_=R[h, c * T_CHUNK : (c + 1) * T_CHUNK, :].rearrange("(r a) k -> r (a k)", a=ROWS_EACH),
                 )
 
         identity = keep.tile([P, P], F32, name="identity")
@@ -160,7 +160,10 @@ def tile_relativepositionsdpa_pa_s_kernel(tc, queries, v_bias, R, out):
 
         def copy_r(h, c):
             piece = r_grouped[:, h, c * T_CHUNK * PACK : (c + 1) * T_CHUNK * PACK]
-            nc.scalar.copy(out=piece.bitcast(F32), in_=r_ts[h, c][:].rearrange("p a r u -> p (a r u)"))
+            nc.scalar.copy(
+                out=piece.bitcast(F32).rearrange("p (r a u) -> p r a u", a=ROWS_EACH, u=PAIR),
+                in_=r_ts[h, c][:].rearrange("p a r u -> p r a u"),
+            )
 
         def quantize_r(h, c):
             cols = slice(c * T_CHUNK, (c + 1) * T_CHUNK)

@@ -41,24 +41,25 @@ def tile_relativepositionsdpa_pa_s_kernel(tc, queries, v_bias, R, out):
     with tc.manual_schedule(), tc.tile_pool(name="keep", bufs=1) as keep, tc.psum_pool(
         name="transposed", bufs=4
     ) as transposed, tc.psum_pool(name="scores", bufs=4) as scores:
+        bias_rows = keep.tile([P, K], BF16, name="bias_rows")
+        nc.vector.memset(bias_rows[:].bitcast(F32), 0.0)
         zeros = keep.tile([P, P], F32, name="zeros")
         nc.vector.memset(zeros[:], 0.0)
         warm = transposed.tile([P, T], F32, tag="t", name="warm")
         nc.tensor.matmul(
-            out=warm[:].rearrange("p (i j) -> p i j", j=P),
+            out=warm[:, 0:384].rearrange("p (i j) -> p i j", j=P),
             lhsT=zeros[:],
-            rhs=zeros[:].unsqueeze(1).to_broadcast([P, T // P, P]),
+            rhs=zeros[:].unsqueeze(1).to_broadcast([P, 3, P]),
             start=True,
             stop=True,
         )
-        bias = keep.tile([P, HEADS, PACK], BF16, name="bias")
         q_pairs = queries.rearrange("(n h) (q a) k -> h q n (a k)", h=HEADS, a=ROWS)
         q_raw = keep.tile([P, HEADS, ROWS * K], BF16, name="q_raw")
         r_raw = keep.tile([P, HEADS, CHUNKS, ROWS_EACH * K], BF16, name="r_raw")
         for h in range(HEADS):
             nc.sync.dma_start(out=q_raw[:, h, :], in_=q_pairs[h])
             if h == 0:
-                nc.sync.dma_start(out=bias[:], in_=v_bias.rearrange("o h i (p t) -> p (o h i) t", t=PACK))
+                nc.sync.dma_start(out=bias_rows[0:HEADS, :], in_=v_bias.rearrange("o h i k -> (o h i) k"))
             for c in range(CHUNKS):
                 nc.sync.dma_start(
                     out=r_raw[:, h, c, :],
@@ -85,6 +86,16 @@ def tile_relativepositionsdpa_pa_s_kernel(tc, queries, v_bias, R, out):
         q_scales = keep.tile([P, HEADS, ROWS * P], U8, name="q_scales", align_bytes=64)
         r_codes = keep.tile([P, HEADS, T], U32, name="r_codes", align_bytes=64)
         r_scales = keep.tile([P, HEADS, T], U8, name="r_scales", align_bytes=64)
+
+        bias_t = transposed.tile([P, PAIR, P], F32, tag="t", name="bias_t")
+        for u in range(PAIR):
+            nc.tensor.transpose(bias_t[:, u, :], bias_rows[:].bitcast(F32)[:, u::PAIR], identity[:])
+        bias_words = keep.tile([P, HEADS * PAIR], F32, name="bias_words")
+        nc.vector.tensor_copy(
+            out=bias_words[:].rearrange("p (h u) -> p h u", u=PAIR),
+            in_=bias_t[:, :, 0:HEADS].rearrange("p u h -> p h u"),
+        )
+        bias_values = bias_words[:].bitcast(BF16)
 
         out_all = out.rearrange("b s t -> (b s t)")
         RUN = ROWS * PADDED
@@ -138,7 +149,7 @@ def tile_relativepositionsdpa_pa_s_kernel(tc, queries, v_bias, R, out):
                 out=q_grouped[:, h, :, :],
                 in0=q_ts[h][:].rearrange("p a c u -> p (a c u)").bitcast(BF16).rearrange("p (g t) -> p g t", t=PACK),
                 scalar=K**-0.5,
-                in1=bias[:, h, :].unsqueeze(1).to_broadcast([P, ROWS * P, PACK]),
+                in1=bias_values[:, h * PACK : (h + 1) * PACK].unsqueeze(1).to_broadcast([P, ROWS * P, PACK]),
                 op0=MULT,
                 op1=ADD,
             )

@@ -264,4 +264,4 @@ def tile_relativepositionsdpa_pa_s_kernel(tc, queries, v_bias, R, out):
         empty_spill()
         for r in range(DUOS):
             store_blocks(nc.sync, 0, r)
-            store_blocks(nc.scalar, 1, r)
+            store_blocks(nc.scalar, 1, (r + DUOS // 2) % DUOS)

@@ -32,6 +32,8 @@ BLOCK = 8
 SPILL = 6
 PITCH = ROWS * PADDED + SPILL
 
+FIRST, LAST = 1, 0
+
 FLOPS = 2 * BATCHES * S * T * K
 BYTES = 2 * (BATCHES * S * K + HEADS * K + HEADS * T * K) + 4 * BATCHES * S * T
 
@@ -39,13 +41,13 @@ BYTES = 2 * (BATCHES * S * K + HEADS * K + HEADS * T * K) + 4 * BATCHES * S * T
 def tile_relativepositionsdpa_pa_s_kernel(tc, queries, v_bias, R, out):
     nc = tc.nc
     with tc.manual_schedule(), tc.tile_pool(name="keep", bufs=1) as keep, tc.psum_pool(
-        name="transposed", bufs=4
+        name="transposed", bufs=2
     ) as transposed, tc.psum_pool(name="scores", bufs=4) as scores:
         bias_rows = keep.tile([P, K], BF16, name="bias_rows")
         nc.vector.memset(bias_rows[:].bitcast(F32), 0.0)
         zeros = keep.tile([P, P], F32, name="zeros")
         nc.vector.memset(zeros[:], 0.0)
-        warm = transposed.tile([P, T], F32, tag="t", name="warm")
+        warm = scores.tile([P, T], F32, tag="pos", name="warm")
         nc.tensor.matmul(
             out=warm[:, 0:384].rearrange("p (i j) -> p i j", j=P),
             lhsT=zeros[:],
@@ -56,9 +58,9 @@ def tile_relativepositionsdpa_pa_s_kernel(tc, queries, v_bias, R, out):
         q_pairs = queries.rearrange("(n h) (q a) k -> h q n (a k)", h=HEADS, a=ROWS)
         q_raw = keep.tile([P, HEADS, ROWS * K], BF16, name="q_raw")
         r_raw = keep.tile([P, HEADS, CHUNKS, ROWS_EACH * K], BF16, name="r_raw")
-        for h in range(HEADS):
+        for h in (FIRST, LAST):
             nc.sync.dma_start(out=q_raw[:, h, :], in_=q_pairs[h])
-            if h == 0:
+            if h == FIRST:
                 nc.sync.dma_start(out=bias_rows[0:HEADS, :], in_=v_bias.rearrange("o h i k -> (o h i) k"))
             for c in range(CHUNKS):
                 nc.sync.dma_start(
@@ -87,7 +89,7 @@ def tile_relativepositionsdpa_pa_s_kernel(tc, queries, v_bias, R, out):
         r_codes = keep.tile([P, HEADS, T], U32, name="r_codes", align_bytes=64)
         r_scales = keep.tile([P, HEADS, T], U8, name="r_scales", align_bytes=64)
 
-        bias_t = transposed.tile([P, PAIR, P], F32, tag="t", name="bias_t")
+        bias_t = scores.tile([P, PAIR, P], F32, tag="pos", name="bias_t")
         for u in range(PAIR):
             nc.tensor.transpose(bias_t[:, u, :], bias_rows[:].bitcast(F32)[:, u::PAIR], identity[:])
         bias_words = keep.tile([P, HEADS * PAIR], F32, name="bias_words")
@@ -104,32 +106,31 @@ def tile_relativepositionsdpa_pa_s_kernel(tc, queries, v_bias, R, out):
             first = first + b * S * T
             return out_all[first : first + count * pitch].rearrange("(q c) -> q c", c=pitch)
 
-        def store_plain(n):
-            b = n * HEADS
-            nc.sync.dma_start(out=runs(b, 0, S // ROWS, RUN)[:, 0 : RUN - DROPPED], in_=padded[n::SEQS, 0, DROPPED:RUN])
+        def store_plain(n, cols):
+            to = runs(n * HEADS + FIRST, -DROPPED, S // ROWS, RUN)
+            nc.sync.dma_start(out=to[:, cols], in_=padded[n::SEQS, FIRST, cols])
 
-        def store_plain_front(n):
-            b = n * HEADS
-            nc.sync.dma_start(
-                out=runs(b, RUN - DROPPED, S // ROWS - 1, RUN)[:, 0:DROPPED],
-                in_=padded[SEQS + n :: SEQS, 0, 0:DROPPED],
-            )
+        def region(b, g, count, at, width):
+            early = 0 if b == 0 else DROPPED
+            shift = at - DROPPED + early
+            if shift < 0:
+                g = g - 1
+                shift = shift + GROUP
+            return runs(b, -early, GROUPS, GROUP)[g : g + count, shift : shift + width]
 
         def store_blocks(queue, n, r):
-            b = n * HEADS + 1
             begin = DROPPED if r == 0 else -(r * RUN) % BLOCK
             end = RUN + -((r + 1) * RUN) % BLOCK
             at = r * RUN
             queue.dma_start(
-                out=runs(b, -DROPPED, GROUPS, GROUP)[:, at + begin : at + end],
-                in_=padded[r * GROUPS * SEQS + n : (r + 1) * GROUPS * SEQS : SEQS, 1, begin:end],
+                out=region(n * HEADS + LAST, 0, GROUPS, at + begin, end - begin),
+                in_=padded[r * GROUPS * SEQS + n : (r + 1) * GROUPS * SEQS : SEQS, LAST, begin:end],
             )
 
         def store_blocks_front(n):
-            b = n * HEADS + 1
             nc.gpsimd.dma_start(
-                out=runs(b, GROUP - DROPPED, GROUPS - 1, GROUP)[:, 0:DROPPED],
-                in_=padded[SEQS + n : GROUPS * SEQS : SEQS, 1, 0:DROPPED],
+                out=region(n * HEADS + LAST, 1, GROUPS - 1, 0, DROPPED),
+                in_=padded[SEQS + n : GROUPS * SEQS : SEQS, LAST, 0:DROPPED],
             )
 
         q_ts = {}
@@ -137,11 +138,11 @@ def tile_relativepositionsdpa_pa_s_kernel(tc, queries, v_bias, R, out):
         poss = {}
 
         def transpose_q(h):
-            q_t = transposed.tile([P, ROWS, P, PAIR], F32, tag="t", name="q_t%d" % h)
+            q_t = transposed.tile([P, ROWS, P, PAIR], F32, tag="q_t", name="q_t%d" % h)
             for a in range(ROWS):
                 q_words = q_raw[:, h, a * K : (a + 1) * K].bitcast(F32)
                 for u in range(PAIR):
-                    nc.tensor.transpose(q_t[:, a, :, u], q_words[:, u::PAIR], (identity, perm)[h][:])
+                    nc.tensor.transpose(q_t[:, a, :, u], q_words[:, u::PAIR], (perm if h == LAST else identity)[:])
             q_ts[h] = q_t
 
         def form_q(h):
@@ -163,7 +164,7 @@ def tile_relativepositionsdpa_pa_s_kernel(tc, queries, v_bias, R, out):
 
         def transpose_r(h, c):
             r_words = r_raw[:, h, c, :].bitcast(F32).rearrange("p (a w) -> p a w", a=ROWS_EACH)
-            r_t = transposed.tile([P, ROWS_EACH, P, PAIR], F32, tag="t", name="r_t%d_%d" % (h, c))
+            r_t = transposed.tile([P, ROWS_EACH, P, PAIR], F32, tag="r_t", name="r_t%d_%d" % (h, c))
             for i in range(ROWS_EACH):
                 for u in range(PAIR):
                     nc.tensor.transpose(r_t[:, i, :, u], r_words[:, i, u::PAIR], identity[:])
@@ -211,56 +212,56 @@ def tile_relativepositionsdpa_pa_s_kernel(tc, queries, v_bias, R, out):
             nc.vector.quantize_mx(
                 out=next_codes[:].bitcast(FP8X4),
                 scales=next_scales[:],
-                in_=q_grouped[:, 1, P // DUOS : P // DUOS + P, :].rearrange("p g t -> p (g t)"),
+                in_=q_grouped[:, LAST, P // DUOS : P // DUOS + P, :].rearrange("p g t -> p (g t)"),
             )
 
         def score_next():
-            spill = transposed.tile([P, 64], F32, tag="t", name="spill")
+            spill = transposed.tile([P, 64], F32, tag="q_t", name="spill")
             poss[1] = spill
-            multiply(spill[:], next_codes[:], next_scales[:], 1, slice(0, 64))
+            multiply(spill[:], next_codes[:], next_scales[:], LAST, slice(0, 64))
 
         def empty_spill():
             first = ROWS * PADDED + 1
-            nc.scalar.copy(out=padded[:, 1, first:PITCH], in_=poss[1][:, 0 : PITCH - first])
+            nc.scalar.copy(out=padded[:, LAST, first:PITCH], in_=poss[1][:, 0 : PITCH - first])
 
-        transpose_q(0)
-        form_q(0)
-        transpose_r(0, 0)
-        copy_r(0, 0)
-        transpose_r(0, 1)
-        copy_r(0, 1)
-        quantize_q(0)
-        quantize_r(0, 0)
-        quantize_r(0, 1)
-        transpose_q(1)
-        form_q(1)
-        transpose_r(1, 0)
-        copy_r(1, 0)
-        score(0, 0)
-        empty(nc.scalar.copy, 0, 0, 0)
-        empty(nc.scalar.copy, 0, 1, 0)
-        store_plain_front(0)
-        store_plain_front(1)
-        transpose_r(1, 1)
-        copy_r(1, 1)
-        score(0, 1)
-        empty(nc.scalar.copy, 0, 0, 1)
-        empty(nc.scalar.copy, 0, 1, 1)
-        store_plain(0)
-        store_plain(1)
-        quantize_r(1, 0)
-        quantize_q(1)
-        quantize_r(1, 1)
+        transpose_q(FIRST)
+        form_q(FIRST)
+        transpose_r(FIRST, 0)
+        copy_r(FIRST, 0)
+        transpose_r(FIRST, 1)
+        copy_r(FIRST, 1)
+        quantize_r(FIRST, 0)
+        quantize_q(FIRST)
+        quantize_r(FIRST, 1)
+        transpose_q(LAST)
+        form_q(LAST)
+        transpose_r(LAST, 0)
+        copy_r(LAST, 0)
+        score(FIRST, 0)
+        empty(nc.scalar.copy, FIRST, 0, 0)
+        empty(nc.scalar.copy, FIRST, 1, 0)
+        store_plain(0, slice(0, DROPPED))
+        store_plain(1, slice(0, DROPPED))
+        transpose_r(LAST, 1)
+        copy_r(LAST, 1)
+        score(FIRST, 1)
+        empty(nc.scalar.copy, FIRST, 0, 1)
+        empty(nc.scalar.copy, FIRST, 1, 1)
+        store_plain(0, slice(DROPPED, RUN))
+        store_plain(1, slice(DROPPED, RUN))
+        quantize_r(LAST, 0)
+        quantize_q(LAST)
+        quantize_r(LAST, 1)
         quantize_next()
-        score(1, 0)
-        empty(nc.vector.tensor_copy, 1, 0, 0)
-        empty(nc.scalar.copy, 1, 1, 0)
+        score(LAST, 0)
+        empty(nc.vector.tensor_copy, LAST, 0, 0)
+        empty(nc.scalar.copy, LAST, 1, 0)
         store_blocks_front(0)
         store_blocks_front(1)
-        score(1, 1)
+        score(LAST, 1)
         score_next()
-        empty(nc.vector.tensor_copy, 1, 0, 1)
-        empty(nc.scalar.copy, 1, 1, 1)
+        empty(nc.vector.tensor_copy, LAST, 0, 1)
+        empty(nc.scalar.copy, LAST, 1, 1)
         empty_spill()
         for r in range(DUOS):
             store_blocks(nc.sync, 0, r)

import concourse.mybir as mybir
from concourse.masks import make_identity

F32 = mybir.dt.float32
BF16 = mybir.dt.bfloat16
U32 = mybir.dt.uint32
U8 = mybir.dt.uint8
FP8X4 = mybir.dt.float8_e4m3fn_x4
MULT = mybir.AluOpType.mult
ADD = mybir.AluOpType.add

P = 128
SEQS = 2
HEADS = 2
BATCHES = SEQS * HEADS
S = 128
T = 512
K = 512
PACK = 4
PAIR = 2
T_CHUNK = 256
CHUNKS = T // T_CHUNK
ROWS_EACH = T_CHUNK // P
PADDED = T + 1
DROPPED = S

GROUPS = 16
DUOS = 4
ROWS = 2
GROUP = DUOS * ROWS * PADDED
BLOCK = 8
SPILL = 6
PITCH = ROWS * PADDED + SPILL

FIRST, LAST = 1, 0

FLOPS = 2 * BATCHES * S * T * K
BYTES = 2 * (BATCHES * S * K + HEADS * K + HEADS * T * K) + 4 * BATCHES * S * T


def tile_relativepositionsdpa_pa_s_kernel(tc, queries, v_bias, R, out):
    nc = tc.nc
    with tc.manual_schedule(), tc.tile_pool(name="keep", bufs=1) as keep, tc.psum_pool(
        name="transposed", bufs=2
    ) as transposed, tc.psum_pool(name="scores", bufs=4) as scores:
        bias_rows = keep.tile([P, K], BF16, name="bias_rows")
        nc.vector.memset(bias_rows[:].bitcast(F32), 0.0)
        zeros = keep.tile([P, P], F32, name="zeros")
        nc.vector.memset(zeros[:], 0.0)
        warm = scores.tile([P, T], F32, tag="pos", name="warm")
        nc.tensor.matmul(
            out=warm[:, 0:384].rearrange("p (i j) -> p i j", j=P),
            lhsT=zeros[:],
            rhs=zeros[:].unsqueeze(1).to_broadcast([P, 3, P]),
            start=True,
            stop=True,
        )
        q_pairs = queries.rearrange("(n h) (q a) k -> h q n (a k)", h=HEADS, a=ROWS)
        q_raw = keep.tile([P, HEADS, ROWS * K], BF16, name="q_raw")
        r_raw = keep.tile([P, HEADS, CHUNKS, ROWS_EACH * K], BF16, name="r_raw")
        for h in (FIRST, LAST):
            nc.sync.dma_start(out=q_raw[:, h, :], in_=q_pairs[h])
            if h == FIRST:
                nc.sync.dma_start(out=bias_rows[0:HEADS, :], in_=v_bias.rearrange("o h i k -> (o h i) k"))
            for c in range(CHUNKS):
                nc.sync.dma_start(
                    out=r_raw[:, h, c, :],
                    in_=R[h, c * T_CHUNK : (c + 1) * T_CHUNK, :].rearrange("(r a) k -> r (a k)", a=ROWS_EACH),
                )

        identity = keep.tile([P, P], F32, name="identity")
        make_identity(nc, identity[:])
        perm = keep.tile([P, P], F32, name="perm")
        nc.vector.tensor_copy(
            out=perm[:].rearrange("p (r g n) -> p r g n", n=SEQS, r=DUOS),
            in_=identity[:].rearrange("p (g r n) -> p r g n", n=SEQS, r=DUOS),
        )

        padded = keep.tile([P, HEADS, PITCH], F32, name="padded")
        for j in range(ROWS + 1):
            nc.vector.memset(padded[:, :, j * PADDED : j * PADDED + 1], 0.0)

        q_grouped = keep.tile([P, HEADS, ROWS * P, PACK], BF16, name="q_grouped", align_bytes=64)
        r_grouped = keep.tile([P, HEADS, T * PACK], BF16, name="r_grouped", align_bytes=64)
        q_codes = keep.tile([P, HEADS, ROWS * P], U32, name="q_codes", align_bytes=64)
        next_codes = keep.tile([P, P], U32, name="next_codes", align_bytes=64)
        next_scales = keep.tile([P, P], U8, name="next_scales", align_bytes=64)
        q_scales = keep.tile([P, HEADS, ROWS * P], U8, name="q_scales", align_bytes=64)
        r_codes = keep.tile([P, HEADS, T], U32, name="r_codes", align_bytes=64)
        r_scales = keep.tile([P, HEADS, T], U8, name="r_scales", align_bytes=64)

        bias_t = scores.tile([P, PAIR, P], F32, tag="pos", name="bias_t")
        for u in range(PAIR):
            nc.tensor.transpose(bias_t[:, u, :], bias_rows[:].bitcast(F32)[:, u::PAIR], identity[:])
        bias_words = keep.tile([P, HEADS * PAIR], F32, name="bias_words")
        nc.vector.tensor_copy(
            out=bias_words[:].rearrange("p (h u) -> p h u", u=PAIR),
            in_=bias_t[:, :, 0:HEADS].rearrange("p u h -> p h u"),
        )
        bias_values = bias_words[:].bitcast(BF16)

        out_all = out.rearrange("b s t -> (b s t)")
        RUN = ROWS * PADDED

        def runs(b, first, count, pitch):
            first = first + b * S * T
            return out_all[first : first + count * pitch].rearrange("(q c) -> q c", c=pitch)

        def store_plain(n, cols):
            to = runs(n * HEADS + FIRST, -DROPPED, S // ROWS, RUN)
            nc.sync.dma_start(out=to[:, cols], in_=padded[n::SEQS, FIRST, cols])

        def region(b, g, count, at, width):
            early = 0 if b == 0 else DROPPED
            shift = at - DROPPED + early
            if shift < 0:
                g = g - 1
                shift = shift + GROUP
            return runs(b, -early, GROUPS, GROUP)[g : g + count, shift : shift + width]

        def store_blocks(queue, n, r):
            begin = DROPPED if r == 0 else -(r * RUN) % BLOCK
            end = RUN + -((r + 1) * RUN) % BLOCK
            at = r * RUN
            queue.dma_start(
                out=region(n * HEADS + LAST, 0, GROUPS, at + begin, end - begin),
                in_=padded[r * GROUPS * SEQS + n : (r + 1) * GROUPS * SEQS : SEQS, LAST, begin:end],
            )

        def store_blocks_front(n):
            nc.gpsimd.dma_start(
                out=region(n * HEADS + LAST, 1, GROUPS - 1, 0, DROPPED),
                in_=padded[SEQS + n : GROUPS * SEQS : SEQS, LAST, 0:DROPPED],
            )

        q_ts = {}
        r_ts = {}
        poss = {}

        def transpose_q(h):
            q_t = transposed.tile([P, ROWS, P, PAIR], F32, tag="q_t", name="q_t%d" % h)
            for a in range(ROWS):
                q_words = q_raw[:, h, a * K : (a + 1) * K].bitcast(F32)
                for u in range(PAIR):
                    nc.tensor.transpose(q_t[:, a, :, u], q_words[:, u::PAIR], (perm if h == LAST else identity)[:])
            q_ts[h] = q_t

        def form_q(h):
            nc.vector.scalar_tensor_tensor(
                out=q_grouped[:, h, :, :],
                in0=q_ts[h][:].rearrange("p a c u -> p (a c u)").bitcast(BF16).rearrange("p (g t) -> p g t", t=PACK),
                scalar=K**-0.5,
                in1=bias_values[:, h * PACK : (h + 1) * PACK].unsqueeze(1).to_broadcast([P, ROWS * P, PACK]),
                op0=MULT,
                op1=ADD,
            )

        def quantize_q(h):
            nc.vector.quantize_mx(
                out=q_codes[:, h, :].bitcast(FP8X4),
                scales=q_scales[:, h, :],
                in_=q_grouped[:, h, :, :].rearrange("p g t -> p (g t)"),
            )

        def transpose_r(h, c):
            r_words = r_raw[:, h, c, :].bitcast(F32).rearrange("p (a w) -> p a w", a=ROWS_EACH)
            r_t = transposed.tile([P, ROWS_EACH, P, PAIR], F32, tag="r_t", name="r_t%d_%d" % (h, c))
            for i in range(ROWS_EACH):
                for u in range(PAIR):
                    nc.tensor.transpose(r_t[:, i, :, u], r_words[:, i, u::PAIR], identity[:])
            r_ts[h, c] = r_t

        def copy_r(h, c):
            piece = r_grouped[:, h, c * T_CHUNK * PACK : (c + 1) * T_CHUNK * PACK]
            nc.scalar.copy(
                out=piece.bitcast(F32).rearrange("p (r a u) -> p r a u", a=ROWS_EACH, u=PAIR),
                in_=r_ts[h, c][:].rearrange("p a r u -> p r a u"),
            )

        def quantize_r(h, c):
            cols = slice(c * T_CHUNK, (c + 1) * T_CHUNK)
            nc.vector.quantize_mx(
                out=r_codes[:, h, cols].bitcast(FP8X4),
                scales=r_scales[:, h, cols],
                in_=r_grouped[:, h, c * T_CHUNK * PACK : (c + 1) * T_CHUNK * PACK],
            )

        def multiply(out_tile, codes, scales, h, cols):
            nc.tensor.matmul_mx(
                out=out_tile,
                lhsT=codes.bitcast(FP8X4),
                lhsT_scale=scales,
                rhs=r_codes[:, h, cols].bitcast(FP8X4),
                rhs_scale=r_scales[:, h, cols],
                start=True,
                stop=True,
            )

        def score(h, c):
            cols = slice(c * T_CHUNK, (c + 1) * T_CHUNK)
            for a in range(ROWS):
                pos = scores.tile([P, T], F32, tag="pos", name="pos%d_%d_%d" % (h, a, c))
                poss[h, a, c] = pos
                own = slice(a * P, (a + 1) * P)
                multiply(pos[:, 0:T_CHUNK], q_codes[:, h, own], q_scales[:, h, own], h, cols)

        def empty(copy, h, a, c):
            first = a * PADDED + 1 + c * T_CHUNK
            copy(out=padded[:, h, first : first + T_CHUNK], in_=poss[h, a, c][:, 0:T_CHUNK])

        def quantize_next():
            nc.vector.quantize_mx(
                out=next_codes[:].bitcast(FP8X4),
                scales=next_scales[:],
                in_=q_grouped[:, LAST, P // DUOS : P // DUOS + P, :].rearrange("p g t -> p (g t)"),
            )

        def score_next():
            spill = transposed.tile([P, 64], F32, tag="q_t", name="spill")
            poss[1] = spill
            multiply(spill[:], next_codes[:], next_scales[:], LAST, slice(0, 64))

        def empty_spill():
            first = ROWS * PADDED + 1
            nc.scalar.copy(out=padded[:, LAST, first:PITCH], in_=poss[1][:, 0 : PITCH - first])

        transpose_q(FIRST)
        form_q(FIRST)
        transpose_r(FIRST, 0)
        copy_r(FIRST, 0)
        transpose_r(FIRST, 1)
        copy_r(FIRST, 1)
        quantize_r(FIRST, 0)
        quantize_q(FIRST)
        quantize_r(FIRST, 1)
        transpose_q(LAST)
        form_q(LAST)
        transpose_r(LAST, 0)
        copy_r(LAST, 0)
        score(FIRST, 0)
        empty(nc.scalar.copy, FIRST, 0, 0)
        empty(nc.scalar.copy, FIRST, 1, 0)
        store_plain(0, slice(0, DROPPED))
        store_plain(1, slice(0, DROPPED))
        transpose_r(LAST, 1)
        copy_r(LAST, 1)
        score(FIRST, 1)
        empty(nc.scalar.copy, FIRST, 0, 1)
        empty(nc.scalar.copy, FIRST, 1, 1)
        store_plain(0, slice(DROPPED, RUN))
        store_plain(1, slice(DROPPED, RUN))
        quantize_r(LAST, 0)
        quantize_q(LAST)
        quantize_r(LAST, 1)
        quantize_next()
        score(LAST, 0)
        empty(nc.vector.tensor_copy, LAST, 0, 0)
        empty(nc.scalar.copy, LAST, 1, 0)
        store_blocks_front(0)
        store_blocks_front(1)
        score(LAST, 1)
        score_next()
        empty(nc.vector.tensor_copy, LAST, 0, 1)
        empty(nc.scalar.copy, LAST, 1, 1)
        empty_spill()
        for r in range(DUOS):
            store_blocks(nc.sync, 0, r)
            store_blocks(nc.scalar, 1, (r + DUOS // 2) % DUOS)
